import numpy as np
import ml_dtypes


def mxq(x, axis, fmt="e4m3"):
    dtype, down = {"e4m3": (ml_dtypes.float8_e4m3fn, 7), "e5m2": (ml_dtypes.float8_e5m2, 14)}[fmt]
    v = np.moveaxis(np.asarray(x, np.float32).astype(ml_dtypes.bfloat16).astype(np.float64), axis, -1)
    blocks = v.reshape(v.shape[:-1] + (-1, 32))
    amax = np.abs(blocks).max(-1, keepdims=True)
    byte = np.maximum(np.where(amax > 0, np.frexp(amax)[1] - 1 + 127, 0) - down, 1)
    scale = np.exp2(byte - 127.0)
    codes = (blocks / scale).astype(np.float32).astype(dtype).astype(np.float64)
    return np.moveaxis((codes * scale).reshape(v.shape), -1, axis)


WIDE = False


def mx_kscale(k):
    if not WIDE:
        return np.ones(k)
    levels = np.array([10, -10, 5, -5, 0])
    a = np.random.permutation(np.resize(levels, k // 512 * 4)).reshape(k // 512, 4)
    idx = np.arange(k)
    return np.exp2(a[idx // 512, idx % 128 // 32])


BF16 = ml_dtypes.bfloat16


def bf(x):
    return np.asarray(x, np.float32).astype(BF16)


def f64(x):
    return np.asarray(x).astype(np.float64)


E2M1 = np.array([0.0, 0.5, 1.0, 1.5, 2.0, 3.0, 4.0, 6.0, -0.0, -0.5, -1.0, -1.5, -2.0, -3.0, -4.0, -6.0])


def pack_weight(w, fmt):
    k, n = w.shape
    w = f64(bf(w)).reshape(k // 32, 32, n)
    amax = np.abs(w).max(1)
    if fmt == "e4m3":
        byte = np.frexp(amax)[1] - 1 + 127 - 7
    else:
        mant, ex = np.frexp(amax / 6.0)
        byte = np.where(mant > 0.5, ex, ex - 1) + 127
    byte = np.clip(np.where(amax > 0, byte, 1), 1, 254)
    scaled = (w * np.exp2(127.0 - byte)[:, None, :]).reshape(k, n).astype(np.float32)
    by_word = np.ascontiguousarray(scaled.reshape(k // 512, 128, 4, n).transpose(0, 1, 3, 2))
    if fmt == "e4m3":
        words = by_word.astype(ml_dtypes.float8_e4m3fn).view(np.uint8)
    else:
        c = by_word.astype(ml_dtypes.float4_e2m1fn).view(np.uint8) & 0xF
        words = c[..., 0::2] | (c[..., 1::2] << 4)
    return np.ascontiguousarray(words), np.ascontiguousarray(byte.astype(np.uint8).reshape(k // 512, 16, n))


def unpack_weight(words, scales, fmt):
    g, p, n, _ = words.shape
    if fmt == "e4m3":
        vals = np.ascontiguousarray(words).view(ml_dtypes.float8_e4m3fn).astype(np.float64)
    else:
        nib = np.empty((g, p, n, 4), np.uint8)
        nib[..., 0::2] = words & 0xF
        nib[..., 1::2] = words >> 4
        vals = E2M1[nib]
    vals = vals * np.repeat(np.exp2(scales.astype(np.float64) - 127.0), 8, axis=1)[..., None]
    return vals.transpose(0, 1, 3, 2).reshape(g * 512, n)


T, D_IN, D_OUT = 128, 4096, 8192


def setup_inputs():
    s = mx_kscale(D_IN)
    x = bf(np.random.standard_normal((T, D_IN)) * s)
    w = np.random.standard_normal((D_IN, D_OUT)) / 64.0 / s[:, None]
    w_words, w_scales = pack_weight(w, "e4m3")
    bias = bf(np.random.standard_normal(D_OUT) * 0.5)
    return {"x": x, "w_words": w_words, "w_scales": w_scales, "bias": bias}


def reference(x, w_words, w_scales, bias):
    w = unpack_weight(w_words, w_scales, "e4m3")
    return (mxq(f64(x), 1, "e4m3") @ w) + f64(bias)[None, :]

@@ -1,0 +1,175 @@
+from contextlib import ExitStack
+
+import concourse.mybir as mybir
+from concourse.masks import make_identity
+
+F32 = mybir.dt.float32
+BF16 = mybir.dt.bfloat16
+I32 = mybir.dt.int32
+U32 = mybir.dt.uint32
+U8 = mybir.dt.uint8
+FP8X4 = mybir.dt.float8_e4m3fn_x4
+
+P = 128
+T, D_IN, D_OUT = 128, 4096, 8192
+K_PASS = 512
+GROUPS = D_IN // K_PASS
+N_TILE = 512
+BANKS = 8
+HALF = BANKS * N_TILE
+W_BUFS = 8
+
+FLOPS = 2 * T * D_IN * D_OUT
+
+
+def tile_linearfp8_kernel(tc, x, w_words, w_scales, bias, out):
+    nc = tc.nc
+    with ExitStack() as ctx:
+        keep = ctx.enter_context(tc.tile_pool(name="keep", bufs=1))
+        wpool = ctx.enter_context(tc.tile_pool(name="wpool", bufs=W_BUFS))
+        psum = ctx.enter_context(tc.psum_pool(name="psum", bufs=1))
+        ctx.enter_context(tc.manual_schedule())
+
+        x_sb = keep.tile([P, D_IN], BF16, name="x_sb")
+        nc.sync.dma_start(out=x_sb[:], in_=x)
+
+        bias_rows = keep.tile([P, N_TILE], BF16, name="bias_rows")
+        nc.vector.memset(bias_rows[:], 0.0)
+        nc.sync.dma_start(
+            out=bias_rows[0 : D_OUT // N_TILE, :],
+            in_=bias.rearrange("(c n) -> c n", n=N_TILE),
+        )
+
+        planes = keep.tile([P, GROUPS // 4, D_OUT], U8, name="planes", align_bytes=64)
+        nc.vector.memset(planes[:].rearrange("p j n -> p (j n)").bitcast(I32), 0)
+
+        ident32 = keep.tile([P, P], F32, name="ident32")
+        make_identity(nc, ident32[:])
+        identb = keep.tile([P, P], BF16, name="identb")
+        make_identity(nc, identb[:])
+
+        scale_rows = w_scales.rearrange("(j k) q n -> k j q n", k=4)
+        for r in range(4):
+            for quad in (0, 2, 1, 3):
+                first = 32 * quad + r
+                nc.gpsimd.dma_start(
+                    out=planes[first : first + 16 : 4, :, :].bitcast(F32),
+                    in_=scale_rows[:, :, 4 * quad + r, :].bitcast(F32),
+                )
+
+        words = w_words.rearrange("g p n t -> p g (n t)")
+        steps = []
+        for g in range(GROUPS):
+            steps.append(((g,), 0, HALF))
+        for g in range(GROUPS - 2):
+            steps.append(((g,), HALF, HALF))
+        steps.append(((GROUPS - 2, GROUPS - 1), HALF, HALF // 2))
+        steps.append(((GROUPS - 2, GROUPS - 1), HALF + HALF // 2, HALF // 2))
+
+        w_tiles = {}
+
+        def load(i):
+            gs, c0, ncols = steps[i]
+            w_t = wpool.tile([P, HALF], U32, name="w_t", tag="w_t", align_bytes=64)
+            w_tiles[i] = w_t
+            if len(gs) == 1:
+                nc.sync.dma_start(
+                    out=w_t[:].bitcast(I32),
+                    in_=words[:, gs[0], 4 * c0 : 4 * (c0 + ncols)].bitcast(I32),
+                )
+            else:
+                nc.sync.dma_start(
+                    out=w_t[:].rearrange("p (g n) -> p g n", g=len(gs)).bitcast(I32),
+                    in_=words[:, gs[0] : gs[-1] + 1, 4 * c0 : 4 * (c0 + ncols)].bitcast(I32),
+                )
+
+        for i in range(W_BUFS):
+            load(i)
+
+        bias_bc = keep.tile([P, D_OUT], BF16, name="bias_bc")
+
+        def spread_bias(i):
+            pb = psum.tile([P, 2 * N_TILE], BF16, name="pb", tag="bank%d" % (4 + i % 4))
+            for s in range(2):
+                c = 2 * i + s
+                nc.tensor.matmul(
+                    out=pb[:, s * N_TILE : (s + 1) * N_TILE],
+                    lhsT=identb[:, c : c + 1].to_broadcast([P, P]),
+                    rhs=bias_rows[:],
+                    start=True,
+                    stop=True,
+                )
+            nc.scalar.copy(out=bias_bc[:, 2 * N_TILE * i : 2 * N_TILE * (i + 1)], in_=pb[:])
+
+        for i in range(4):
+            spread_bias(i)
+
+        x_words = x_sb[:].bitcast(F32)
+        grouped = keep.tile([P, D_IN], BF16, name="grouped", align_bytes=64)
+        grouped_words = grouped[:].bitcast(F32).rearrange("p (g m u) -> p g m u", g=GROUPS, u=2)
+        for pair in range(GROUPS // 2):
+            xt = psum.tile([P, 2, 2, T], F32, name="xt", tag="bank%d" % pair)
+            for gl in range(2):
+                g = 2 * pair + gl
+                for u in range(2):
+                    nc.tensor.transpose(
+                        xt[:, gl, u, :],
+                        x_words[:, 256 * g + u : 256 * (g + 1) : 2],
+                        ident32[:],
+                    )
+            nc.vector.tensor_copy(
+                out=grouped_words[:, 2 * pair : 2 * pair + 2, :, :],
+                in_=xt[:].rearrange("p g u m -> p g m u"),
+            )
+        x_codes = keep.tile([P, GROUPS * T], U32, name="x_codes", align_bytes=64)
+        x_scales = keep.tile([P, GROUPS * T], U8, name="x_scales", align_bytes=64)
+        for hq in range(2):
+            cols = slice(hq * 4 * T, (hq + 1) * 4 * T)
+            nc.vector.quantize_mx(
+                out=x_codes[:, cols].bitcast(FP8X4),
+                scales=x_scales[:, cols],
+                in_=grouped[:, hq * 16 * T : (hq + 1) * 16 * T],
+            )
+
+        for i in range(4, 8):
+            spread_bias(i)
+
+        out_sb = [keep.tile([P, HALF], F32, name="out_sb%d" % h) for h in range(2)]
+        acc = {}
+        for i in range(len(steps)):
+            gs, c0, ncols = steps[i]
+            w_t = w_tiles[i]
+            for blk in range(ncols // N_TILE):
+                col = c0 + blk * N_TILE
+                b = (col // N_TILE) % BANKS
+                for gi in range(len(gs)):
+                    g = gs[gi]
+                    if g == 0:
+                        acc[b] = psum.tile([P, N_TILE], F32, name="acc", tag="bank%d" % b)
+                    w0 = gi * ncols + blk * N_TILE
+                    nc.tensor.matmul_mx(
+                        out=acc[b][:],
+                        lhsT=x_codes[:, g * T : (g + 1) * T].bitcast(FP8X4),
+                        lhsT_scale=x_scales[:, g * T : (g + 1) * T],
+                        rhs=w_t[:, w0 : w0 + N_TILE].bitcast(FP8X4),
+                        rhs_scale=planes[4 * (g % 4) : P, g // 4, col : col + N_TILE],
+                        start=(g == 0),
+                        stop=(g == GROUPS - 1),
+                    )
+                    if g == GROUPS - 1:
+                        h = col // HALF
+                        nc.vector.tensor_tensor(
+                            out=out_sb[h][:, col - h * HALF : col - h * HALF + N_TILE],
+                            in0=acc[b][:],
+                            in1=bias_bc[:, col : col + N_TILE],
+                            op=mybir.AluOpType.add,
+                        )
+            if i + W_BUFS < len(steps):
+                load(i + W_BUFS)
+
+        for c0, ncols in ((0, 4096), (4096, 2048), (6144, 1024), (7168, 512), (7680, 512)):
+            h = c0 // HALF
+            nc.sync.dma_start(
+                out=out[:, c0 : c0 + ncols],
+                in_=out_sb[h][:, c0 - h * HALF : c0 - h * HALF + ncols],
+            )

@@ -48,13 +48,11 @@ def tile_linearfp8_kernel(tc, x, w_words, w_scales, bias, out):
         identb = keep.tile([P, P], BF16, name="identb")
         make_identity(nc, identb[:])
 
-        scale_rows = w_scales.rearrange("(j k) q n -> k j q n", k=4)
-        for r in range(4):
-            for quad in (0, 2, 1, 3):
-                first = 32 * quad + r
-                nc.gpsimd.dma_start(
-                    out=planes[first : first + 16 : 4, :, :].bitcast(F32),
-                    in_=scale_rows[:, :, 4 * quad + r, :].bitcast(F32),
+        for j in range(GROUPS // 4):
+            for quad in range(4):
+                nc.sync.dma_start(
+                    out=planes[32 * quad : 32 * quad + 16, j, :].bitcast(I32),
+                    in_=w_scales[4 * j : 4 * j + 4, 4 * quad : 4 * quad + 4, :].bitcast(I32),
                 )
 
         words = w_words.rearrange("g p n t -> p g (n t)")

@@ -48,11 +48,13 @@ def tile_linearfp8_kernel(tc, x, w_words, w_scales, bias, out):
         identb = keep.tile([P, P], BF16, name="identb")
         make_identity(nc, identb[:])
 
-        for j in range(GROUPS // 4):
-            for quad in range(4):
-                nc.sync.dma_start(
-                    out=planes[32 * quad : 32 * quad + 16, j, :].bitcast(I32),
-                    in_=w_scales[4 * j : 4 * j + 4, 4 * quad : 4 * quad + 4, :].bitcast(I32),
+        scale_rows = w_scales.rearrange("(j k) q n -> k j q n", k=4)
+        for r in range(4):
+            for quad in (0, 3, 2, 1):
+                first = 32 * quad + r
+                nc.gpsimd.dma_start(
+                    out=planes[first : first + 16 : 4, :, :].bitcast(F32),
+                    in_=scale_rows[:, :, 4 * quad + r, :].bitcast(F32),
                 )
 
         words = w_words.rearrange("g p n t -> p g (n t)")

@@ -61,10 +61,11 @@ def tile_linearfp8_kernel(tc, x, w_words, w_scales, bias, out):
         steps = []
         for g in range(GROUPS):
             steps.append(((g,), 0, HALF))
-        for g in range(GROUPS - 2):
+        for g in range(GROUPS - 1):
             steps.append(((g,), HALF, HALF))
-        steps.append(((GROUPS - 2, GROUPS - 1), HALF, HALF // 2))
-        steps.append(((GROUPS - 2, GROUPS - 1), HALF + HALF // 2, HALF // 2))
+        steps.append(((GROUPS - 1,), HALF, 2048))
+        steps.append(((GROUPS - 1,), HALF + 2048, 1024))
+        steps.append(((GROUPS - 1,), HALF + 3072, 1024))
 
         w_tiles = {}
 
@@ -72,16 +73,10 @@ def tile_linearfp8_kernel(tc, x, w_words, w_scales, bias, out):
             gs, c0, ncols = steps[i]
             w_t = wpool.tile([P, HALF], U32, name="w_t", tag="w_t", align_bytes=64)
             w_tiles[i] = w_t
-            if len(gs) == 1:
-                nc.sync.dma_start(
-                    out=w_t[:].bitcast(I32),
-                    in_=words[:, gs[0], 4 * c0 : 4 * (c0 + ncols)].bitcast(I32),
-                )
-            else:
-                nc.sync.dma_start(
-                    out=w_t[:].rearrange("p (g n) -> p g n", g=len(gs)).bitcast(I32),
-                    in_=words[:, gs[0] : gs[-1] + 1, 4 * c0 : 4 * (c0 + ncols)].bitcast(I32),
-                )
+            nc.sync.dma_start(
+                out=w_t[:, 0:ncols].bitcast(I32),
+                in_=words[:, gs[0], 4 * c0 : 4 * (c0 + ncols)].bitcast(I32),
+            )
 
         for i in range(W_BUFS):
             load(i)
@@ -167,7 +162,7 @@ def tile_linearfp8_kernel(tc, x, w_words, w_scales, bias, out):
             if i + W_BUFS < len(steps):
                 load(i + W_BUFS)
 
-        for c0, ncols in ((0, 4096), (4096, 2048), (6144, 1024), (7168, 512), (7680, 512)):
+        for c0, ncols in ((0, 4096), (4096, 2048), (6144, 1024), (7168, 1024)):
             h = c0 // HALF
             nc.sync.dma_start(
                 out=out[:, c0 : c0 + ncols],

@@ -48,13 +48,11 @@ def tile_linearfp8_kernel(tc, x, w_words, w_scales, bias, out):
         identb = keep.tile([P, P], BF16, name="identb")
         make_identity(nc, identb[:])
 
-        scale_rows = w_scales.rearrange("(j k) q n -> k j q n", k=4)
-        for r in range(4):
+        for j in range(GROUPS // 4):
             for quad in (0, 3, 2, 1):
-                first = 32 * quad + r
                 nc.gpsimd.dma_start(
-                    out=planes[first : first + 16 : 4, :, :].bitcast(F32),
-                    in_=scale_rows[:, :, 4 * quad + r, :].bitcast(F32),
+                    out=planes[32 * quad : 32 * quad + 16, j, :].bitcast(F32),
+                    in_=w_scales[4 * j : 4 * j + 4, 4 * quad : 4 * quad + 4, :].bitcast(F32),
                 )
 
         words = w_words.rearrange("g p n t -> p g (n t)")

@@ -48,11 +48,13 @@ def tile_linearfp8_kernel(tc, x, w_words, w_scales, bias, out):
         identb = keep.tile([P, P], BF16, name="identb")
         make_identity(nc, identb[:])
 
-        for j in range(GROUPS // 4):
+        scale_rows = w_scales.rearrange("(j k) q n -> k j q n", k=4)
+        for r in range(4):
             for quad in (0, 3, 2, 1):
+                first = 32 * quad + r
                 nc.gpsimd.dma_start(
-                    out=planes[32 * quad : 32 * quad + 16, j, :].bitcast(F32),
-                    in_=w_scales[4 * j : 4 * j + 4, 4 * quad : 4 * quad + 4, :].bitcast(F32),
+                    out=planes[first : first + 16 : 4, :, :].bitcast(F32),
+                    in_=scale_rows[:, :, 4 * quad + r, :].bitcast(F32),
                 )
 
         words = w_words.rearrange("g p n t -> p g (n t)")
@@ -159,8 +161,10 @@ def tile_linearfp8_kernel(tc, x, w_words, w_scales, bias, out):
                         )
             if i + W_BUFS < len(steps):
                 load(i + W_BUFS)
+            if i == GROUPS - 1:
+                nc.scalar.dma_start(out=out[:, 0:HALF], in_=out_sb[0][:])
 
-        for c0, ncols in ((0, 4096), (4096, 2048), (6144, 1024), (7168, 1024)):
+        for c0, ncols in ((4096, 2048), (6144, 1024), (7168, 1024)):
             h = c0 // HALF
             nc.sync.dma_start(
                 out=out[:, c0 : c0 + ncols],

from contextlib import ExitStack

import concourse.mybir as mybir
from concourse.masks import make_identity

F32 = mybir.dt.float32
BF16 = mybir.dt.bfloat16
I32 = mybir.dt.int32
U32 = mybir.dt.uint32
U8 = mybir.dt.uint8
FP8X4 = mybir.dt.float8_e4m3fn_x4

P = 128
T, D_IN, D_OUT = 128, 4096, 8192
K_PASS = 512
GROUPS = D_IN // K_PASS
N_TILE = 512
BANKS = 8
HALF = BANKS * N_TILE
W_BUFS = 8

FLOPS = 2 * T * D_IN * D_OUT


def tile_linearfp8_kernel(tc, x, w_words, w_scales, bias, out):
    nc = tc.nc
    with ExitStack() as ctx:
        keep = ctx.enter_context(tc.tile_pool(name="keep", bufs=1))
        wpool = ctx.enter_context(tc.tile_pool(name="wpool", bufs=W_BUFS))
        psum = ctx.enter_context(tc.psum_pool(name="psum", bufs=1))
        ctx.enter_context(tc.manual_schedule())

        x_sb = keep.tile([P, D_IN], BF16, name="x_sb")
        nc.sync.dma_start(out=x_sb[:], in_=x)

        bias_rows = keep.tile([P, N_TILE], BF16, name="bias_rows")
        nc.vector.memset(bias_rows[:], 0.0)
        nc.sync.dma_start(
            out=bias_rows[0 : D_OUT // N_TILE, :],
            in_=bias.rearrange("(c n) -> c n", n=N_TILE),
        )

        planes = keep.tile([P, GROUPS // 4, D_OUT], U8, name="planes", align_bytes=64)
        nc.vector.memset(planes[:].rearrange("p j n -> p (j n)").bitcast(I32), 0)

        ident32 = keep.tile([P, P], F32, name="ident32")
        make_identity(nc, ident32[:])
        identb = keep.tile([P, P], BF16, name="identb")
        make_identity(nc, identb[:])

        scale_rows = w_scales.rearrange("(j k) q n -> k j q n", k=4)
        for r in range(4):
            for quad in (0, 3, 2, 1):
                first = 32 * quad + r
                nc.gpsimd.dma_start(
                    out=planes[first : first + 16 : 4, :, :].bitcast(F32),
                    in_=scale_rows[:, :, 4 * quad + r, :].bitcast(F32),
                )

        words = w_words.rearrange("g p n t -> p g (n t)")
        steps = []
        for g in range(GROUPS):
            steps.append(((g,), 0, HALF))
        for g in range(GROUPS - 1):
            steps.append(((g,), HALF, HALF))
        steps.append(((GROUPS - 1,), HALF, 2048))
        steps.append(((GROUPS - 1,), HALF + 2048, 1024))
        steps.append(((GROUPS - 1,), HALF + 3072, 1024))

        w_tiles = {}

        def load(i):
            gs, c0, ncols = steps[i]
            w_t = wpool.tile([P, HALF], U32, name="w_t", tag="w_t", align_bytes=64)
            w_tiles[i] = w_t
            nc.sync.dma_start(
                out=w_t[:, 0:ncols].bitcast(I32),
                in_=words[:, gs[0], 4 * c0 : 4 * (c0 + ncols)].bitcast(I32),
            )

        for i in range(W_BUFS):
            load(i)

        bias_bc = keep.tile([P, D_OUT], BF16, name="bias_bc")

        def spread_bias(i):
            pb = psum.tile([P, 2 * N_TILE], BF16, name="pb", tag="bank%d" % (4 + i % 4))
            for s in range(2):
                c = 2 * i + s
                nc.tensor.matmul(
                    out=pb[:, s * N_TILE : (s + 1) * N_TILE],
                    lhsT=identb[:, c : c + 1].to_broadcast([P, P]),
                    rhs=bias_rows[:],
                    start=True,
                    stop=True,
                )
            nc.scalar.copy(out=bias_bc[:, 2 * N_TILE * i : 2 * N_TILE * (i + 1)], in_=pb[:])

        for i in range(4):
            spread_bias(i)

        x_words = x_sb[:].bitcast(F32)
        grouped = keep.tile([P, D_IN], BF16, name="grouped", align_bytes=64)
        grouped_words = grouped[:].bitcast(F32).rearrange("p (g m u) -> p g m u", g=GROUPS, u=2)
        for pair in range(GROUPS // 2):
            xt = psum.tile([P, 2, 2, T], F32, name="xt", tag="bank%d" % pair)
            for gl in range(2):
                g = 2 * pair + gl
                for u in range(2):
                    nc.tensor.transpose(
                        xt[:, gl, u, :],
                        x_words[:, 256 * g + u : 256 * (g + 1) : 2],
                        ident32[:],
                    )
            nc.vector.tensor_copy(
                out=grouped_words[:, 2 * pair : 2 * pair + 2, :, :],
                in_=xt[:].rearrange("p g u m -> p g m u"),
            )
        x_codes = keep.tile([P, GROUPS * T], U32, name="x_codes", align_bytes=64)
        x_scales = keep.tile([P, GROUPS * T], U8, name="x_scales", align_bytes=64)
        for hq in range(2):
            cols = slice(hq * 4 * T, (hq + 1) * 4 * T)
            nc.vector.quantize_mx(
                out=x_codes[:, cols].bitcast(FP8X4),
                scales=x_scales[:, cols],
                in_=grouped[:, hq * 16 * T : (hq + 1) * 16 * T],
            )

        for i in range(4, 8):
            spread_bias(i)

        out_sb = [keep.tile([P, HALF], F32, name="out_sb%d" % h) for h in range(2)]
        acc = {}
        for i in range(len(steps)):
            gs, c0, ncols = steps[i]
            w_t = w_tiles[i]
            for blk in range(ncols // N_TILE):
                col = c0 + blk * N_TILE
                b = (col // N_TILE) % BANKS
                for gi in range(len(gs)):
                    g = gs[gi]
                    if g == 0:
                        acc[b] = psum.tile([P, N_TILE], F32, name="acc", tag="bank%d" % b)
                    w0 = gi * ncols + blk * N_TILE
                    nc.tensor.matmul_mx(
                        out=acc[b][:],
                        lhsT=x_codes[:, g * T : (g + 1) * T].bitcast(FP8X4),
                        lhsT_scale=x_scales[:, g * T : (g + 1) * T],
                        rhs=w_t[:, w0 : w0 + N_TILE].bitcast(FP8X4),
                        rhs_scale=planes[4 * (g % 4) : P, g // 4, col : col + N_TILE],
                        start=(g == 0),
                        stop=(g == GROUPS - 1),
                    )
                    if g == GROUPS - 1:
                        h = col // HALF
                        nc.vector.tensor_tensor(
                            out=out_sb[h][:, col - h * HALF : col - h * HALF + N_TILE],
                            in0=acc[b][:],
                            in1=bias_bc[:, col : col + N_TILE],
                            op=mybir.AluOpType.add,
                        )
            if i + W_BUFS < len(steps):
                load(i + W_BUFS)
            if i == GROUPS - 1:
                nc.scalar.dma_start(out=out[:, 0:HALF], in_=out_sb[0][:])

        for c0, ncols in ((4096, 2048), (6144, 1024), (7168, 1024)):
            h = c0 // HALF
            nc.sync.dma_start(
                out=out[:, c0 : c0 + ncols],
                in_=out_sb[h][:, c0 - h * HALF : c0 - h * HALF + ncols],
            )
